import numpy as np
import ml_dtypes


def mxq(x, axis, fmt="e4m3"):
    dtype, down = {"e4m3": (ml_dtypes.float8_e4m3fn, 7), "e5m2": (ml_dtypes.float8_e5m2, 14)}[fmt]
    v = np.moveaxis(np.asarray(x, np.float32).astype(ml_dtypes.bfloat16).astype(np.float64), axis, -1)
    blocks = v.reshape(v.shape[:-1] + (-1, 32))
    amax = np.abs(blocks).max(-1, keepdims=True)
    byte = np.maximum(np.where(amax > 0, np.frexp(amax)[1] - 1 + 127, 0) - down, 1)
    scale = np.exp2(byte - 127.0)
    codes = (blocks / scale).astype(np.float32).astype(dtype).astype(np.float64)
    return np.moveaxis((codes * scale).reshape(v.shape), -1, axis)


WIDE = False


def mx_kscale(k):
    if not WIDE:
        return np.ones(k)
    levels = np.array([10, -10, 5, -5, 0])
    a = np.random.permutation(np.resize(levels, k // 512 * 4)).reshape(k // 512, 4)
    idx = np.arange(k)
    return np.exp2(a[idx // 512, idx % 128 // 32])


BF16 = ml_dtypes.bfloat16


def bf(x):
    return np.asarray(x, np.float32).astype(BF16)


def f64(x):
    return np.asarray(x).astype(np.float64)


E2M1 = np.array([0.0, 0.5, 1.0, 1.5, 2.0, 3.0, 4.0, 6.0, -0.0, -0.5, -1.0, -1.5, -2.0, -3.0, -4.0, -6.0])


def pack_weight(w, fmt):
    k, n = w.shape
    w = f64(bf(w)).reshape(k // 32, 32, n)
    amax = np.abs(w).max(1)
    if fmt == "e4m3":
        byte = np.frexp(amax)[1] - 1 + 127 - 7
    else:
        mant, ex = np.frexp(amax / 6.0)
        byte = np.where(mant > 0.5, ex, ex - 1) + 127
    byte = np.clip(np.where(amax > 0, byte, 1), 1, 254)
    scaled = (w * np.exp2(127.0 - byte)[:, None, :]).reshape(k, n).astype(np.float32)
    by_word = np.ascontiguousarray(scaled.reshape(k // 512, 128, 4, n).transpose(0, 1, 3, 2))
    if fmt == "e4m3":
        words = by_word.astype(ml_dtypes.float8_e4m3fn).view(np.uint8)
    else:
        c = by_word.astype(ml_dtypes.float4_e2m1fn).view(np.uint8) & 0xF
        words = c[..., 0::2] | (c[..., 1::2] << 4)
    return np.ascontiguousarray(words), np.ascontiguousarray(byte.astype(np.uint8).reshape(k // 512, 16, n))


def unpack_weight(words, scales, fmt):
    g, p, n, _ = words.shape
    if fmt == "e4m3":
        vals = np.ascontiguousarray(words).view(ml_dtypes.float8_e4m3fn).astype(np.float64)
    else:
        nib = np.empty((g, p, n, 4), np.uint8)
        nib[..., 0::2] = words & 0xF
        nib[..., 1::2] = words >> 4
        vals = E2M1[nib]
    vals = vals * np.repeat(np.exp2(scales.astype(np.float64) - 127.0), 8, axis=1)[..., None]
    return vals.transpose(0, 1, 3, 2).reshape(g * 512, n)


S, B, ND, NS, HN, BT, C, Hd, Wd = 8, 16, 32, 96, 512, 16384, 3, 16, 32
P = C * Hd * Wd
EPS = 1e-9
SELU_ALPHA = 1.6732632423543772848170429916717
SELU_SCALE = 1.0507009873554804934193349852946


def selu(v):
    return SELU_SCALE * np.where(v > 0, v, SELU_ALPHA * np.expm1(np.minimum(v, 0.0)))


def sigmoid(v):
    return 1.0 / (1.0 + np.exp(-v))


def setup_inputs():
    t = mx_kscale(HN)
    digits = bf(np.random.random_sample((S, B, ND)))
    styles = bf(np.random.standard_normal((S, B, NS)))
    images = bf(np.random.random_sample((S, B, C, Hd, Wd)))
    W_h = bf(np.random.standard_normal((ND + NS, HN)) / np.sqrt(ND + NS) * t)
    b_h = bf(np.random.standard_normal(HN) * 0.5 * t)
    W1_words, W1_scales = pack_weight(np.random.standard_normal((HN, BT)) * 1.4 / np.sqrt(HN) / t[:, None], "e4m3")
    b1 = bf(np.random.standard_normal(BT) * 0.5)
    W2_words, W2_scales = pack_weight(np.random.standard_normal((BT, P)) / np.sqrt(BT), "e4m3")
    b2 = bf(np.random.standard_normal(P) * 0.5)
    return {"digits": digits,
            "styles": styles,
            "images": images,
            "W_h": W_h,
            "b_h": b_h,
            "W1_words": W1_words,
            "W1_scales": W1_scales,
            "b1": b1,
            "W2_words": W2_words,
            "W2_scales": W2_scales,
            "b2": b2}


def reference(digits, styles, images, W_h, b_h, W1_words, W1_scales, b1, W2_words, W2_scales, b2):
    h = np.maximum(np.concatenate([f64(digits), f64(styles)], axis=-1) @ f64(W_h) + f64(b_h), 0.0)
    t = selu((mxq(h, 2, "e4m3") @ unpack_weight(W1_words, W1_scales, "e4m3")) + f64(b1))
    x_hat = sigmoid((mxq(t, 2, "e4m3") @ unpack_weight(W2_words, W2_scales, "e4m3")) + f64(b2))
    images_mean = x_hat.reshape(x_hat.shape[0], x_hat.shape[1], C, Hd, Wd)
    img = f64(images)
    loss = -(np.log(images_mean + EPS) * img + np.log(1.0 - images_mean + EPS) * (1.0 - img)).sum(-1)
    return loss

@@ -1,0 +1,294 @@
+import math
+from contextlib import ExitStack
+
+import concourse.mybir as mybir
+from concourse.masks import make_identity
+
+F32 = mybir.dt.float32
+BF16 = mybir.dt.bfloat16
+I32 = mybir.dt.int32
+U32 = mybir.dt.uint32
+U8 = mybir.dt.uint8
+FP8X4 = mybir.dt.float8_e4m3fn_x4
+ACT = mybir.ActivationFunctionType
+ALU = mybir.AluOpType
+AXIS = mybir.AxisListType
+
+P = 128
+PACK = 4
+K_PASS = P * PACK
+BANK = 512
+HIDDEN = 512
+UNITS = 16384
+PIXELS = 1536
+ROW = 32
+GROUPS = UNITS // K_PASS
+EPS = 1e-9
+
+SELU_ALPHA = 1.6732632423543772848170429916717
+SELU_SCALE = 1.0507009873554804934193349852946
+SELU_FLOOR = SELU_SCALE * SELU_ALPHA
+
+PLANES = 4
+W1_CHUNK = 2048
+PIXELS_A = 1024
+GROUPS_PER_LOAD_A = 2
+GROUPS_PER_LOAD_B = 4
+STREAM_BUFS = 8
+LAG = 12
+
+ROW_BH = GROUPS
+ROW_B2 = GROUPS + 1
+
+FLOPS = 2 * P * (P * HIDDEN + HIDDEN * UNITS + UNITS * PIXELS)
+
+
+def tile_decoder_k_kernel(
+    tc, digits, styles, images, W_h, b_h, W1_words, W1_scales, b1, W2_words, W2_scales, b2, out
+):
+    nc = tc.nc
+    with ExitStack() as ctx:
+        keep = ctx.enter_context(tc.tile_pool(name="keep", bufs=1))
+        stream = ctx.enter_context(tc.tile_pool(name="stream", bufs=STREAM_BUFS))
+        work = ctx.enter_context(tc.tile_pool(name="work", bufs=3))
+        psum_acc = ctx.enter_context(tc.psum_pool(name="psum_acc", bufs=1))
+        psum_u = ctx.enter_context(tc.psum_pool(name="psum_u", bufs=2))
+        psum_t = ctx.enter_context(tc.psum_pool(name="psum_t", bufs=3))
+
+        w1_dram = W1_words[0].rearrange("p n t -> p (n t)").bitcast(I32)
+        w1_scales_dram = W1_scales[0].bitcast(I32)
+        w2_dram = W2_words.rearrange("g p n t -> p g (n t)").bitcast(I32)
+        w2_scales_dram = W2_scales.bitcast(F32)
+
+        ident_f32 = keep.tile([P, P], F32)
+        make_identity(nc, ident_f32[:])
+        ident_bf = keep.tile([P, P], BF16)
+        make_identity(nc, ident_bf[:])
+        eps_col = keep.tile([P, 1], F32)
+        nc.vector.memset(eps_col[:], EPS)
+
+        w1_planes = keep.tile([P, UNITS // PLANES], U8, align_bytes=64)
+        w2_planes = keep.tile([P, GROUPS // PLANES, PIXELS], U8, align_bytes=64)
+        bias_rows = keep.tile([P, K_PASS], BF16)
+        nc.vector.memset(w1_planes[:].bitcast(I32), 0)
+        nc.vector.memset(bias_rows[:], 0.0)
+        nc.vector.memset(w2_planes[:].bitcast(I32), 0)
+
+        cat_sb = keep.tile([P, P], BF16)
+        n_digits = digits.shape[2]
+        nc.scalar.dma_start(out=cat_sb[:, 0:n_digits], in_=digits.rearrange("s b d -> (s b) d"))
+        nc.scalar.dma_start(out=cat_sb[:, n_digits:P], in_=styles.rearrange("s b d -> (s b) d"))
+        wh_sb = keep.tile([P, HIDDEN], BF16)
+        nc.scalar.dma_start(out=wh_sb[:], in_=W_h)
+        nc.scalar.dma_start(out=bias_rows[0:GROUPS, :], in_=b1.rearrange("(g k) -> g k", k=K_PASS))
+        nc.scalar.dma_start(out=bias_rows[ROW_BH : ROW_BH + 1, :], in_=b_h.rearrange("(g k) -> g k", k=K_PASS))
+        nc.scalar.dma_start(
+            out=bias_rows[ROW_B2 : ROW_B2 + PIXELS // K_PASS, :], in_=b2.rearrange("(g k) -> g k", k=K_PASS)
+        )
+        img_sb = keep.tile([P, PIXELS], BF16)
+        nc.scalar.dma_start(out=img_sb[:], in_=images.rearrange("s b c h w -> (s b) (c h w)"))
+
+        w1_words = keep.tile([P, UNITS], U32, align_bytes=64)
+
+        def load_w1_chunk(c):
+            cols = slice(c * W1_CHUNK, (c + 1) * W1_CHUNK)
+            nc.sync.dma_start(out=w1_words[:, cols].bitcast(I32), in_=w1_dram[:, cols])
+
+        load_w1_chunk(0)
+        for quad in range(4):
+            nc.sync.dma_start(
+                out=w1_planes[32 * quad : 32 * quad + 16, :].bitcast(I32),
+                in_=w1_scales_dram[4 * quad : 4 * quad + 4, :].rearrange("r (k c) -> k r c", k=PLANES),
+            )
+        for c in range(1, UNITS // W1_CHUNK):
+            load_w1_chunk(c)
+
+        for s in range(GROUPS // PLANES):
+            for quad in range(4):
+                nc.gpsimd.dma_start(
+                    out=w2_planes[32 * quad : 32 * quad + 16, s, :].bitcast(F32),
+                    in_=w2_scales_dram[PLANES * s : PLANES * (s + 1), 4 * quad : 4 * quad + 4, :],
+                )
+
+        loads = []
+        for first in range(0, GROUPS, GROUPS_PER_LOAD_A):
+            loads.append((first, GROUPS_PER_LOAD_A, 0, PIXELS_A))
+        for first in range(0, GROUPS, GROUPS_PER_LOAD_B):
+            loads.append((first, GROUPS_PER_LOAD_B, PIXELS_A, PIXELS - PIXELS_A))
+        w2_tiles = {}
+
+        def load_w2(i):
+            if i >= len(loads):
+                return
+            first, n_groups, pixel0, n_pixels = loads[i]
+            w2_tile = stream.tile([P, n_groups, n_pixels], U32, name="w2_tile", tag="w2", align_bytes=64)
+            nc.sync.dma_start(
+                out=w2_tile[:].bitcast(I32),
+                in_=w2_dram[:, first : first + n_groups, pixel0 : pixel0 + n_pixels],
+            )
+            w2_tiles[i] = w2_tile
+
+        for i in range(STREAM_BUFS):
+            load_w2(i)
+
+        bias_sorted = keep.tile([P, PACK, P], BF16)
+        nc.vector.tensor_copy(out=bias_sorted[:], in_=bias_rows[:].rearrange("g (p j) -> g j p", j=PACK))
+        bias_ps = psum_t.tile([P, PACK, P], BF16, name="bias_ps", tag="uT_ps")
+        for j in range(PACK):
+            nc.tensor.transpose(bias_ps[:, j, :], bias_sorted[:, j, :], ident_bf[:])
+        b1_exp = keep.tile([P, PACK, GROUPS], F32)
+        nc.vector.tensor_scalar(
+            out=b1_exp[:], in0=bias_ps[:, :, 0:GROUPS], scalar1=math.log(SELU_FLOOR), scalar2=None, op0=ALU.add
+        )
+        b1_relu = keep.tile([P, PACK, GROUPS], F32)
+        nc.vector.tensor_scalar(
+            out=b1_relu[:], in0=bias_ps[:, :, 0:GROUPS], scalar1=SELU_SCALE, scalar2=None, op0=ALU.mult
+        )
+        bh_col = keep.tile([P, PACK], F32)
+        nc.vector.tensor_copy(out=bh_col[:], in_=bias_ps[:, :, ROW_BH])
+
+        b2_all = keep.tile([P, PIXELS], F32)
+        for i in range(PIXELS // BANK):
+            b2_ps = psum_u.tile([P, BANK], F32, name="b2_ps", tag="u_ps")
+            nc.tensor.matmul(
+                out=b2_ps[:],
+                lhsT=ident_bf[:, ROW_B2 + i : ROW_B2 + i + 1].to_broadcast([P, P]),
+                rhs=bias_rows[:],
+                start=True,
+                stop=True,
+            )
+            nc.scalar.copy(out=b2_all[:, i * BANK : (i + 1) * BANK], in_=b2_ps[:])
+
+        cat_ps = psum_t.tile([P, P], BF16, name="cat_ps", tag="uT_ps")
+        nc.tensor.transpose(cat_ps[:], cat_sb[:], ident_bf[:])
+        catT_sb = keep.tile([P, P], BF16)
+        nc.vector.tensor_copy(out=catT_sb[:], in_=cat_ps[:])
+        wh_sorted = keep.tile([P, PACK, P], BF16)
+        nc.vector.tensor_copy(out=wh_sorted[:], in_=wh_sb[:].rearrange("c (p j) -> c j p", j=PACK))
+        h_ps = psum_t.tile([P, PACK, P], F32, name="h_ps", tag="uT_ps")
+        for j in range(PACK):
+            nc.tensor.matmul(out=h_ps[:, j, :], lhsT=wh_sorted[:, j, :], rhs=catT_sb[:], start=True, stop=True)
+        h_f32 = keep.tile([P, PACK, P], F32)
+        for j in range(PACK):
+            nc.vector.tensor_scalar(
+                out=h_f32[:, j, :], in0=h_ps[:, j, :], scalar1=bh_col[:, j : j + 1], scalar2=0.0,
+                op0=ALU.add, op1=ALU.max,
+            )
+        h_bf = keep.tile([P, P, PACK], BF16, align_bytes=64)
+        nc.vector.tensor_copy(out=h_bf[:], in_=h_f32[:].rearrange("p j m -> p m j"))
+        h_codes = keep.tile([P, P], U32, align_bytes=64)
+        h_plane = keep.tile([P, P], U8, align_bytes=64)
+        nc.vector.quantize_mx(
+            out=h_codes[:].bitcast(FP8X4), scales=h_plane[:], in_=h_bf[:].rearrange("p m j -> p (m j)")
+        )
+
+        t_codes = keep.tile([P, GROUPS, P], U32, align_bytes=64)
+        t_planes = keep.tile([P, GROUPS, P], U8, align_bytes=64)
+        units_per_plane = UNITS // PLANES
+
+        def make_t(g):
+            unit0 = g * K_PASS
+            offset = 4 * (unit0 // units_per_plane)
+            col0 = unit0 % units_per_plane
+            u_ps = psum_u.tile([P, BANK], F32, name="u_ps", tag="u_ps")
+            nc.tensor.matmul_mx(
+                out=u_ps[:],
+                lhsT=h_codes[:].bitcast(FP8X4),
+                lhsT_scale=h_plane[:],
+                rhs=w1_words[:, unit0 : unit0 + K_PASS].bitcast(FP8X4),
+                rhs_scale=w1_planes[offset:P, col0 : col0 + K_PASS],
+                start=True,
+                stop=True,
+            )
+            u_sb = work.tile([P, PACK, P], F32, name="u_sb")
+            nc.vector.tensor_scalar(
+                out=u_sb[:], in0=u_ps[:].rearrange("m (p j) -> m j p", j=PACK),
+                scalar1=SELU_SCALE, scalar2=None, op0=ALU.mult,
+            )
+            uT_ps = psum_t.tile([P, PACK, P], F32, name="uT_ps", tag="uT_ps")
+            for j in range(PACK):
+                nc.tensor.transpose(uT_ps[:, j, :], u_sb[:, j, :], ident_f32[:])
+            e_sb = work.tile([P, PACK, P], F32, name="e_sb")
+            r_sb = work.tile([P, PACK, P], F32, name="r_sb")
+            for j in range(PACK):
+                nc.scalar.activation(
+                    out=e_sb[:, j, :], in_=uT_ps[:, j, :], func=ACT.Exp,
+                    bias=b1_exp[:, j, g : g + 1], scale=1.0 / SELU_SCALE,
+                )
+                nc.scalar.activation(
+                    out=r_sb[:, j, :], in_=uT_ps[:, j, :], func=ACT.Relu, bias=b1_relu[:, j, g : g + 1], scale=1.0,
+                )
+            t_bf = work.tile([P, P, PACK], BF16, name="t_bf", align_bytes=64)
+            nc.vector.scalar_tensor_tensor(
+                out=t_bf[:],
+                in0=e_sb[:].rearrange("p j m -> p m j"),
+                scalar=SELU_FLOOR,
+                in1=r_sb[:].rearrange("p j m -> p m j"),
+                op0=ALU.subtract,
+                op1=ALU.min,
+            )
+            nc.vector.quantize_mx(
+                out=t_codes[:, g, :].bitcast(FP8X4),
+                scales=t_planes[:, g, :],
+                in_=t_bf[:].rearrange("p m j -> p (m j)"),
+            )
+
+        acc = []
+        for bank in range(PIXELS // BANK):
+            acc.append(psum_acc.tile([P, BANK], F32, name="acc%d" % bank))
+
+        def multiply(i):
+            first, n_groups, pixel0, n_pixels = loads[i]
+            for gi in range(n_groups):
+                g = first + gi
+                for col0 in range(0, n_pixels, BANK):
+                    pixel = pixel0 + col0
+                    nc.tensor.matmul_mx(
+                        out=acc[pixel // BANK][:],
+                        lhsT=t_codes[:, g, :].bitcast(FP8X4),
+                        lhsT_scale=t_planes[:, g, :],
+                        rhs=w2_tiles[i][:, gi, col0 : col0 + BANK].bitcast(FP8X4),
+                        rhs_scale=w2_planes[4 * (g % PLANES) : P, g // PLANES, pixel : pixel + BANK],
+                        start=(g == 0),
+                        stop=(g == GROUPS - 1),
+                    )
+            load_w2(i + STREAM_BUFS)
+
+        loss = keep.tile([P, PIXELS // ROW], F32)
+
+        def loss_of(banks):
+            on, off = {}, {}
+            for bank in banks:
+                cols = slice(bank * BANK, (bank + 1) * BANK)
+                z = keep.tile([P, BANK], F32, name="z%d" % bank)
+                nc.vector.tensor_tensor(out=z[:], in0=acc[bank][:], in1=b2_all[:, cols], op=ALU.add)
+                on[bank] = keep.tile([P, BANK], F32, name="on%d" % bank)
+                off[bank] = keep.tile([P, BANK], F32, name="off%d" % bank)
+                nc.scalar.activation(out=on[bank][:], in_=z[:], func=ACT.Sigmoid)
+                nc.scalar.activation(out=off[bank][:], in_=z[:], func=ACT.Sigmoid, scale=-1.0)
+            for bank in banks:
+                cols = slice(bank * BANK, (bank + 1) * BANK)
+                nc.scalar.activation(out=on[bank][:], in_=on[bank][:], func=ACT.Ln, bias=eps_col[:])
+                nc.scalar.activation(out=off[bank][:], in_=off[bank][:], func=ACT.Ln, bias=eps_col[:])
+                nc.vector.tensor_tensor(out=on[bank][:], in0=off[bank][:], in1=on[bank][:], op=ALU.subtract)
+                nc.vector.tensor_tensor(out=on[bank][:], in0=on[bank][:], in1=img_sb[:, cols], op=ALU.mult)
+                nc.vector.tensor_tensor(out=on[bank][:], in0=on[bank][:], in1=off[bank][:], op=ALU.subtract)
+                nc.vector.tensor_reduce(
+                    out=loss[:, bank * (BANK // ROW) : (bank + 1) * (BANK // ROW)],
+                    in_=on[bank][:].rearrange("m (r w) -> m r w", w=ROW),
+                    axis=AXIS.X,
+                    op=ALU.add,
+                )
+
+        n_loads_a = GROUPS // GROUPS_PER_LOAD_A
+        for step in range(GROUPS + LAG):
+            if step < GROUPS:
+                make_t(step)
+            g_done = step - LAG
+            if g_done >= 0 and g_done % GROUPS_PER_LOAD_A == GROUPS_PER_LOAD_A - 1:
+                multiply(g_done // GROUPS_PER_LOAD_A)
+        loss_of(range(PIXELS_A // BANK))
+        for i in range(n_loads_a, len(loads)):
+            multiply(i)
+        loss_of(range(PIXELS_A // BANK, PIXELS // BANK))
+        nc.sync.dma_start(out=out.rearrange("s b c h -> (s b) (c h)"), in_=loss[:])

@@ -31,11 +31,13 @@ SELU_FLOOR = SELU_SCALE * SELU_ALPHA
 
 PLANES = 4
 W1_CHUNK = 2048
+W1_PLANE_COLS = 1024
 PIXELS_A = 1024
-GROUPS_PER_LOAD_A = 2
-GROUPS_PER_LOAD_B = 4
-STREAM_BUFS = 8
-LAG = 12
+GROUPS_WHOLE = 14
+GROUPS_PER_END_LOAD = 2
+GROUPS_LAST = 2
+STREAM_BUFS = 12
+LAG = 8
 
 ROW_BH = GROUPS
 ROW_B2 = GROUPS + 1
@@ -52,16 +54,14 @@ def tile_decoder_k_kernel(
         stream = ctx.enter_context(tc.tile_pool(name="stream", bufs=STREAM_BUFS))
         work = ctx.enter_context(tc.tile_pool(name="work", bufs=3))
         psum_acc = ctx.enter_context(tc.psum_pool(name="psum_acc", bufs=1))
-        psum_u = ctx.enter_context(tc.psum_pool(name="psum_u", bufs=2))
-        psum_t = ctx.enter_context(tc.psum_pool(name="psum_t", bufs=3))
+        psum_b = ctx.enter_context(tc.psum_pool(name="psum_b", bufs=2))
+        psum_u = ctx.enter_context(tc.psum_pool(name="psum_u", bufs=3))
 
         w1_dram = W1_words[0].rearrange("p n t -> p (n t)").bitcast(I32)
         w1_scales_dram = W1_scales[0].bitcast(I32)
         w2_dram = W2_words.rearrange("g p n t -> p g (n t)").bitcast(I32)
         w2_scales_dram = W2_scales.bitcast(F32)
 
-        ident_f32 = keep.tile([P, P], F32)
-        make_identity(nc, ident_f32[:])
         ident_bf = keep.tile([P, P], BF16)
         make_identity(nc, ident_bf[:])
         eps_col = keep.tile([P, 1], F32)
@@ -87,6 +87,7 @@ def tile_decoder_k_kernel(
         )
         img_sb = keep.tile([P, PIXELS], BF16)
         nc.scalar.dma_start(out=img_sb[:], in_=images.rearrange("s b c h w -> (s b) (c h w)"))
+        img_off = keep.tile([P, PIXELS], F32)
 
         w1_words = keep.tile([P, UNITS], U32, align_bytes=64)
 
@@ -95,12 +96,13 @@ def tile_decoder_k_kernel(
             nc.sync.dma_start(out=w1_words[:, cols].bitcast(I32), in_=w1_dram[:, cols])
 
         load_w1_chunk(0)
+        load_w1_chunk(1)
         for quad in range(4):
             nc.sync.dma_start(
                 out=w1_planes[32 * quad : 32 * quad + 16, :].bitcast(I32),
                 in_=w1_scales_dram[4 * quad : 4 * quad + 4, :].rearrange("r (k c) -> k r c", k=PLANES),
             )
-        for c in range(1, UNITS // W1_CHUNK):
+        for c in range(2, UNITS // W1_CHUNK):
             load_w1_chunk(c)
 
         for s in range(GROUPS // PLANES):
@@ -111,10 +113,14 @@ def tile_decoder_k_kernel(
                 )
 
         loads = []
-        for first in range(0, GROUPS, GROUPS_PER_LOAD_A):
-            loads.append((first, GROUPS_PER_LOAD_A, 0, PIXELS_A))
-        for first in range(0, GROUPS, GROUPS_PER_LOAD_B):
-            loads.append((first, GROUPS_PER_LOAD_B, PIXELS_A, PIXELS - PIXELS_A))
+        for g in range(GROUPS_WHOLE):
+            loads.append((g, 1, 0, PIXELS))
+        for g in range(GROUPS_WHOLE, GROUPS):
+            loads.append((g, 1, 0, PIXELS_A))
+        for first in range(GROUPS_WHOLE, GROUPS - GROUPS_LAST, GROUPS_PER_END_LOAD):
+            loads.append((first, GROUPS_PER_END_LOAD, PIXELS_A, BANK))
+        for pixel0 in range(PIXELS_A, PIXELS, BANK // 2):
+            loads.append((GROUPS - GROUPS_LAST, GROUPS_LAST, pixel0, BANK // 2))
         w2_tiles = {}
 
         def load_w2(i):
@@ -133,7 +139,7 @@ def tile_decoder_k_kernel(
 
         bias_sorted = keep.tile([P, PACK, P], BF16)
         nc.vector.tensor_copy(out=bias_sorted[:], in_=bias_rows[:].rearrange("g (p j) -> g j p", j=PACK))
-        bias_ps = psum_t.tile([P, PACK, P], BF16, name="bias_ps", tag="uT_ps")
+        bias_ps = psum_u.tile([P, PACK, P], BF16, name="bias_ps", tag="u_ps")
         for j in range(PACK):
             nc.tensor.transpose(bias_ps[:, j, :], bias_sorted[:, j, :], ident_bf[:])
         b1_exp = keep.tile([P, PACK, GROUPS], F32)
@@ -149,7 +155,7 @@ def tile_decoder_k_kernel(
 
         b2_all = keep.tile([P, PIXELS], F32)
         for i in range(PIXELS // BANK):
-            b2_ps = psum_u.tile([P, BANK], F32, name="b2_ps", tag="u_ps")
+            b2_ps = psum_b.tile([P, BANK], F32, name="b2_ps", tag="b_ps")
             nc.tensor.matmul(
                 out=b2_ps[:],
                 lhsT=ident_bf[:, ROW_B2 + i : ROW_B2 + i + 1].to_broadcast([P, P]),
@@ -159,13 +165,13 @@ def tile_decoder_k_kernel(
             )
             nc.scalar.copy(out=b2_all[:, i * BANK : (i + 1) * BANK], in_=b2_ps[:])
 
-        cat_ps = psum_t.tile([P, P], BF16, name="cat_ps", tag="uT_ps")
+        cat_ps = psum_u.tile([P, P], BF16, name="cat_ps", tag="u_ps")
         nc.tensor.transpose(cat_ps[:], cat_sb[:], ident_bf[:])
         catT_sb = keep.tile([P, P], BF16)
         nc.vector.tensor_copy(out=catT_sb[:], in_=cat_ps[:])
         wh_sorted = keep.tile([P, PACK, P], BF16)
         nc.vector.tensor_copy(out=wh_sorted[:], in_=wh_sb[:].rearrange("c (p j) -> c j p", j=PACK))
-        h_ps = psum_t.tile([P, PACK, P], F32, name="h_ps", tag="uT_ps")
+        h_ps = psum_u.tile([P, PACK, P], F32, name="h_ps", tag="u_ps")
         for j in range(PACK):
             nc.tensor.matmul(out=h_ps[:, j, :], lhsT=wh_sorted[:, j, :], rhs=catT_sb[:], start=True, stop=True)
         h_f32 = keep.tile([P, PACK, P], F32)
@@ -184,40 +190,51 @@ def tile_decoder_k_kernel(
 
         t_codes = keep.tile([P, GROUPS, P], U32, align_bytes=64)
         t_planes = keep.tile([P, GROUPS, P], U8, align_bytes=64)
+        w1_planes_sorted = keep.tile([P, UNITS // PLANES], U8, align_bytes=64)
         units_per_plane = UNITS // PLANES
+
+        def sort_w1_planes(col0):
+            cols = slice(col0, col0 + W1_PLANE_COLS)
+            nc.vector.tensor_copy(
+                out=w1_planes_sorted[:, cols].rearrange("q (g j p) -> q g j p", j=PACK, p=P),
+                in_=w1_planes[:, cols].rearrange("q (g p j) -> q g j p", j=PACK, p=P),
+            )
+
+        r_last = {}
 
         def make_t(g):
             unit0 = g * K_PASS
             offset = 4 * (unit0 // units_per_plane)
             col0 = unit0 % units_per_plane
-            u_ps = psum_u.tile([P, BANK], F32, name="u_ps", tag="u_ps")
-            nc.tensor.matmul_mx(
-                out=u_ps[:],
-                lhsT=h_codes[:].bitcast(FP8X4),
-                lhsT_scale=h_plane[:],
-                rhs=w1_words[:, unit0 : unit0 + K_PASS].bitcast(FP8X4),
-                rhs_scale=w1_planes[offset:P, col0 : col0 + K_PASS],
-                start=True,
-                stop=True,
+            if unit0 < units_per_plane and col0 % W1_PLANE_COLS == 0:
+                sort_w1_planes(col0)
+            w1_sorted = work.tile([P, PACK, P], U32, name="w1_sorted", align_bytes=64)
+            nc.vector.tensor_copy(
+                out=w1_sorted[:].bitcast(I32),
+                in_=w1_words[:, unit0 : unit0 + K_PASS].bitcast(I32).rearrange("q (p j) -> q j p", j=PACK),
             )
-            u_sb = work.tile([P, PACK, P], F32, name="u_sb")
-            nc.vector.tensor_scalar(
-                out=u_sb[:], in0=u_ps[:].rearrange("m (p j) -> m j p", j=PACK),
-                scalar1=SELU_SCALE, scalar2=None, op0=ALU.mult,
-            )
-            uT_ps = psum_t.tile([P, PACK, P], F32, name="uT_ps", tag="uT_ps")
+            u_ps = psum_u.tile([P, PACK, P], F32, name="u_ps", tag="u_ps")
             for j in range(PACK):
-                nc.tensor.transpose(uT_ps[:, j, :], u_sb[:, j, :], ident_f32[:])
+                nc.tensor.matmul_mx(
+                    out=u_ps[:, j, :],
+                    lhsT=w1_sorted[:, j, :].bitcast(FP8X4),
+                    lhsT_scale=w1_planes_sorted[offset:P, col0 + j * P : col0 + (j + 1) * P],
+                    rhs=h_codes[:].bitcast(FP8X4),
+                    rhs_scale=h_plane[:],
+                    start=True,
+                    stop=True,
+                )
             e_sb = work.tile([P, PACK, P], F32, name="e_sb")
             r_sb = work.tile([P, PACK, P], F32, name="r_sb")
             for j in range(PACK):
                 nc.scalar.activation(
-                    out=e_sb[:, j, :], in_=uT_ps[:, j, :], func=ACT.Exp,
-                    bias=b1_exp[:, j, g : g + 1], scale=1.0 / SELU_SCALE,
+                    out=e_sb[:, j, :], in_=u_ps[:, j, :], func=ACT.Exp, bias=b1_exp[:, j, g : g + 1], scale=1.0
                 )
                 nc.scalar.activation(
-                    out=r_sb[:, j, :], in_=uT_ps[:, j, :], func=ACT.Relu, bias=b1_relu[:, j, g : g + 1], scale=1.0,
+                    out=r_sb[:, j, :], in_=u_ps[:, j, :], func=ACT.Relu, bias=b1_relu[:, j, g : g + 1],
+                    scale=SELU_SCALE,
                 )
+            r_last[0] = r_sb
             t_bf = work.tile([P, P, PACK], BF16, name="t_bf", align_bytes=64)
             nc.vector.scalar_tensor_tensor(
                 out=t_bf[:],
@@ -236,59 +253,97 @@ def tile_decoder_k_kernel(
         acc = []
         for bank in range(PIXELS // BANK):
             acc.append(psum_acc.tile([P, BANK], F32, name="acc%d" % bank))
+        acc_last = {}
 
         def multiply(i):
             first, n_groups, pixel0, n_pixels = loads[i]
             for gi in range(n_groups):
                 g = first + gi
-                for col0 in range(0, n_pixels, BANK):
+                width = min(n_pixels, BANK)
+                for col0 in range(0, n_pixels, width):
                     pixel = pixel0 + col0
+                    if width == BANK:
+                        acc_cols = acc[pixel // BANK][:]
+                        g_start, g_stop = 0, GROUPS - 1 if pixel < PIXELS_A else GROUPS - GROUPS_LAST - 1
+                    else:
+                        acc_cols = acc_last[pixel][:, 0:width]
+                        g_start, g_stop = GROUPS - GROUPS_LAST, GROUPS - 1
                     nc.tensor.matmul_mx(
-                        out=acc[pixel // BANK][:],
+                        out=acc_cols,
                         lhsT=t_codes[:, g, :].bitcast(FP8X4),
                         lhsT_scale=t_planes[:, g, :],
-                        rhs=w2_tiles[i][:, gi, col0 : col0 + BANK].bitcast(FP8X4),
-                        rhs_scale=w2_planes[4 * (g % PLANES) : P, g // PLANES, pixel : pixel + BANK],
-                        start=(g == 0),
-                        stop=(g == GROUPS - 1),
+                        rhs=w2_tiles[i][:, gi, col0 : col0 + width].bitcast(FP8X4),
+                        rhs_scale=w2_planes[4 * (g % PLANES) : P, g // PLANES, pixel : pixel + width],
+                        start=(g == g_start),
+                        stop=(g == g_stop),
                     )
             load_w2(i + STREAM_BUFS)
 
         loss = keep.tile([P, PIXELS // ROW], F32)
+        sums = keep.tile([P, PIXELS // ROW], F32)
+        on = keep.tile([P, PIXELS], F32)
+        off = keep.tile([P, PIXELS], F32)
 
-        def loss_of(banks):
-            on, off = {}, {}
-            for bank in banks:
-                cols = slice(bank * BANK, (bank + 1) * BANK)
-                z = keep.tile([P, BANK], F32, name="z%d" % bank)
-                nc.vector.tensor_tensor(out=z[:], in0=acc[bank][:], in1=b2_all[:, cols], op=ALU.add)
-                on[bank] = keep.tile([P, BANK], F32, name="on%d" % bank)
-                off[bank] = keep.tile([P, BANK], F32, name="off%d" % bank)
-                nc.scalar.activation(out=on[bank][:], in_=z[:], func=ACT.Sigmoid)
-                nc.scalar.activation(out=off[bank][:], in_=z[:], func=ACT.Sigmoid, scale=-1.0)
-            for bank in banks:
-                cols = slice(bank * BANK, (bank + 1) * BANK)
-                nc.scalar.activation(out=on[bank][:], in_=on[bank][:], func=ACT.Ln, bias=eps_col[:])
-                nc.scalar.activation(out=off[bank][:], in_=off[bank][:], func=ACT.Ln, bias=eps_col[:])
-                nc.vector.tensor_tensor(out=on[bank][:], in0=off[bank][:], in1=on[bank][:], op=ALU.subtract)
-                nc.vector.tensor_tensor(out=on[bank][:], in0=on[bank][:], in1=img_sb[:, cols], op=ALU.mult)
-                nc.vector.tensor_tensor(out=on[bank][:], in0=on[bank][:], in1=off[bank][:], op=ALU.subtract)
-                nc.vector.tensor_reduce(
-                    out=loss[:, bank * (BANK // ROW) : (bank + 1) * (BANK // ROW)],
-                    in_=on[bank][:].rearrange("m (r w) -> m r w", w=ROW),
-                    axis=AXIS.X,
-                    op=ALU.add,
-                )
+        def loss_sigmoid(c0, n, sums_ps):
+            cols = slice(c0, c0 + n)
+            nc.vector.tensor_tensor(out=off[:, cols], in0=sums_ps, in1=b2_all[:, cols], op=ALU.add)
+            nc.scalar.activation(out=on[:, cols], in_=off[:, cols], func=ACT.Sigmoid)
+            nc.scalar.activation(out=off[:, cols], in_=off[:, cols], func=ACT.Sigmoid, scale=-1.0)
 
-        n_loads_a = GROUPS // GROUPS_PER_LOAD_A
-        for step in range(GROUPS + LAG):
-            if step < GROUPS:
-                make_t(step)
-            g_done = step - LAG
-            if g_done >= 0 and g_done % GROUPS_PER_LOAD_A == GROUPS_PER_LOAD_A - 1:
-                multiply(g_done // GROUPS_PER_LOAD_A)
-        loss_of(range(PIXELS_A // BANK))
-        for i in range(n_loads_a, len(loads)):
-            multiply(i)
-        loss_of(range(PIXELS_A // BANK, PIXELS // BANK))
-        nc.sync.dma_start(out=out.rearrange("s b c h -> (s b) (c h)"), in_=loss[:])
+        def loss_log(c0, n):
+            cols = slice(c0, c0 + n)
+            nc.scalar.activation(out=on[:, cols], in_=on[:, cols], func=ACT.Ln, bias=eps_col[:])
+            nc.scalar.activation(out=off[:, cols], in_=off[:, cols], func=ACT.Ln, bias=eps_col[:])
+
+        def loss_sum(c0, n):
+            cols = slice(c0, c0 + n)
+            rows = slice(c0 // ROW, (c0 + n) // ROW)
+            nc.vector.tensor_tensor(out=on[:, cols], in0=on[:, cols], in1=img_sb[:, cols], op=ALU.mult)
+            nc.vector.tensor_reduce(
+                out=sums[:, rows], in_=on[:, cols].rearrange("m (r w) -> m r w", w=ROW), axis=AXIS.X, op=ALU.add
+            )
+            nc.vector.tensor_tensor(out=off[:, cols], in0=off[:, cols], in1=img_off[:, cols], op=ALU.mult)
+            nc.vector.tensor_reduce(
+                out=loss[:, rows], in_=off[:, cols].rearrange("m (r w) -> m r w", w=ROW), axis=AXIS.X, op=ALU.add
+            )
+            nc.vector.scalar_tensor_tensor(
+                out=loss[:, rows], in0=loss[:, rows], scalar=-1.0, in1=sums[:, rows], op0=ALU.mult, op1=ALU.subtract
+            )
+
+        with tc.manual_schedule(engines={mybir.EngineType.PE}):
+            for step in range(GROUPS + LAG):
+                if step < GROUPS:
+                    make_t(step)
+                g_done = step - LAG
+                if g_done >= 0:
+                    multiply(g_done)
+        nc.vector.tensor_scalar(
+            out=img_off[:], in0=img_sb[:], scalar1=-1.0, scalar2=1.0, op0=ALU.mult, op1=ALU.add
+        )
+        table_sb = keep.tile([P, 1], F32)
+        nc.scalar.activation(out=table_sb[:], in_=r_last[0][:, 0, 0:1], func=ACT.Sigmoid)
+        with tc.manual_schedule(engines={mybir.EngineType.PE, mybir.EngineType.Activation, mybir.EngineType.DVE}):
+            pieces = [(0, BANK), (BANK, BANK)]
+            for c0, n in pieces:
+                loss_sigmoid(c0, n, acc[c0 // BANK][:])
+            for c0, n in pieces:
+                loss_log(c0, n)
+            nc.scalar.activation(out=table_sb[:], in_=off[:, PIXELS_A - 1 : PIXELS_A], func=ACT.Sigmoid)
+            for c0, n in pieces:
+                loss_sum(c0, n)
+            for i in range(GROUPS, len(loads) - 2):
+                multiply(i)
+            b2_last = b2_all[:, PIXELS_A:PIXELS]
+            nc.vector.tensor_tensor(out=b2_last, in0=acc[PIXELS_A // BANK][:], in1=b2_last, op=ALU.add)
+            pieces = [(PIXELS_A, BANK // 2), (PIXELS_A + BANK // 2, BANK // 2)]
+            for c0, n in pieces:
+                acc_last[c0] = psum_b.tile([P, BANK], F32, name="acc_last", tag="b_ps")
+            multiply(len(loads) - 2)
+            multiply(len(loads) - 1)
+            for c0, n in pieces:
+                loss_sigmoid(c0, n, acc_last[c0][:, 0:n])
+            for c0, n in pieces:
+                loss_log(c0, n)
+            for c0, n in pieces:
+                loss_sum(c0, n)
+            nc.sync.dma_start(out=out.rearrange("s b c h -> (s b) (c h)"), in_=loss[:])

@@ -72,7 +72,8 @@ def tile_decoder_k_kernel(
         bias_rows = keep.tile([P, K_PASS], BF16)
         nc.vector.memset(w1_planes[:].bitcast(I32), 0)
         nc.vector.memset(bias_rows[:], 0.0)
-        nc.vector.memset(w2_planes[:].bitcast(I32), 0)
+        for i in range(GROUPS // PLANES):
+            nc.vector.memset(w2_planes[:, i, :].bitcast(I32), 0)
 
         cat_sb = keep.tile([P, P], BF16)
         n_digits = digits.shape[2]
@@ -200,54 +201,66 @@ def tile_decoder_k_kernel(
                 in_=w1_planes[:, cols].rearrange("q (g p j) -> q g j p", j=PACK, p=P),
             )
 
-        r_last = {}
+        sorted_tiles, u_tiles, e_tiles, r_tiles, t_tiles, in_tiles = {}, {}, {}, {}, {}, {}
 
-        def make_t(g):
+        def sort_w1(g):
             unit0 = g * K_PASS
-            offset = 4 * (unit0 // units_per_plane)
-            col0 = unit0 % units_per_plane
-            if unit0 < units_per_plane and col0 % W1_PLANE_COLS == 0:
-                sort_w1_planes(col0)
+            if unit0 < units_per_plane and unit0 % W1_PLANE_COLS == 0:
+                sort_w1_planes(unit0)
             w1_sorted = work.tile([P, PACK, P], U32, name="w1_sorted", align_bytes=64)
             nc.vector.tensor_copy(
                 out=w1_sorted[:].bitcast(I32),
                 in_=w1_words[:, unit0 : unit0 + K_PASS].bitcast(I32).rearrange("q (p j) -> q j p", j=PACK),
             )
+            sorted_tiles[g] = w1_sorted
+
+        def project(g):
+            unit0 = g * K_PASS
+            offset = 4 * (unit0 // units_per_plane)
+            col0 = unit0 % units_per_plane
             u_ps = psum_u.tile([P, PACK, P], F32, name="u_ps", tag="u_ps")
             for j in range(PACK):
                 nc.tensor.matmul_mx(
                     out=u_ps[:, j, :],
-                    lhsT=w1_sorted[:, j, :].bitcast(FP8X4),
+                    lhsT=sorted_tiles[g][:, j, :].bitcast(FP8X4),
                     lhsT_scale=w1_planes_sorted[offset:P, col0 + j * P : col0 + (j + 1) * P],
                     rhs=h_codes[:].bitcast(FP8X4),
                     rhs_scale=h_plane[:],
                     start=True,
                     stop=True,
                 )
+            u_tiles[g] = u_ps
+
+        def activate(g):
             e_sb = work.tile([P, PACK, P], F32, name="e_sb")
-            r_sb = work.tile([P, PACK, P], F32, name="r_sb")
+            r_sb = work.tile([P, PACK, P], BF16, name="r_sb")
             for j in range(PACK):
                 nc.scalar.activation(
-                    out=e_sb[:, j, :], in_=u_ps[:, j, :], func=ACT.Exp, bias=b1_exp[:, j, g : g + 1], scale=1.0
+                    out=e_sb[:, j, :], in_=u_tiles[g][:, j, :], func=ACT.Exp, bias=b1_exp[:, j, g : g + 1], scale=1.0
                 )
                 nc.scalar.activation(
-                    out=r_sb[:, j, :], in_=u_ps[:, j, :], func=ACT.Relu, bias=b1_relu[:, j, g : g + 1],
+                    out=r_sb[:, j, :], in_=u_tiles[g][:, j, :], func=ACT.Relu, bias=b1_relu[:, j, g : g + 1],
                     scale=SELU_SCALE,
                 )
-            r_last[0] = r_sb
-            t_bf = work.tile([P, P, PACK], BF16, name="t_bf", align_bytes=64)
+            e_tiles[g], r_tiles[g] = e_sb, r_sb
+
+        def join(g):
+            t_bf = work.tile([P, PACK, P], BF16, name="t_bf")
             nc.vector.scalar_tensor_tensor(
-                out=t_bf[:],
-                in0=e_sb[:].rearrange("p j m -> p m j"),
-                scalar=SELU_FLOOR,
-                in1=r_sb[:].rearrange("p j m -> p m j"),
-                op0=ALU.subtract,
-                op1=ALU.min,
+                out=t_bf[:], in0=e_tiles[g][:], scalar=SELU_FLOOR, in1=r_tiles[g][:], op0=ALU.subtract, op1=ALU.min
             )
+            t_tiles[g] = t_bf
+
+        def interleave(g):
+            t_in = work.tile([P, P, PACK], BF16, name="t_in", align_bytes=64)
+            nc.vector.tensor_copy(out=t_in[:], in_=t_tiles[g][:].rearrange("p j m -> p m j"))
+            in_tiles[g] = t_in
+
+        def quantize(g):
             nc.vector.quantize_mx(
                 out=t_codes[:, g, :].bitcast(FP8X4),
                 scales=t_planes[:, g, :],
-                in_=t_bf[:].rearrange("p m j -> p (m j)"),
+                in_=in_tiles[g][:].rearrange("p m j -> p (m j)"),
             )
 
         acc = []
@@ -310,18 +323,30 @@ def tile_decoder_k_kernel(
                 out=loss[:, rows], in0=loss[:, rows], scalar=-1.0, in1=sums[:, rows], op0=ALU.mult, op1=ALU.subtract
             )
 
-        with tc.manual_schedule(engines={mybir.EngineType.PE}):
+        with tc.manual_schedule(engines={mybir.EngineType.PE, mybir.EngineType.Activation, mybir.EngineType.DVE}):
+            sort_w1(0)
+            sort_w1(1)
+            project(0)
             for step in range(GROUPS + LAG):
+                if step + 1 < GROUPS:
+                    project(step + 1)
                 if step < GROUPS:
-                    make_t(step)
-                g_done = step - LAG
-                if g_done >= 0:
-                    multiply(g_done)
+                    activate(step)
+                if 0 <= step - 1 < GROUPS:
+                    join(step - 1)
+                if 0 <= step - 2 < GROUPS:
+                    quantize(step - 2)
+                if step + 2 < GROUPS:
+                    sort_w1(step + 2)
+                if 0 <= step - 1 < GROUPS:
+                    interleave(step - 1)
+                if step - LAG >= 0:
+                    multiply(step - LAG)
         nc.vector.tensor_scalar(
             out=img_off[:], in0=img_sb[:], scalar1=-1.0, scalar2=1.0, op0=ALU.mult, op1=ALU.add
         )
         table_sb = keep.tile([P, 1], F32)
-        nc.scalar.activation(out=table_sb[:], in_=r_last[0][:, 0, 0:1], func=ACT.Sigmoid)
+        nc.scalar.activation(out=table_sb[:], in_=e_tiles[GROUPS - 1][:, 0, 0:1], func=ACT.Sigmoid)
         with tc.manual_schedule(engines={mybir.EngineType.PE, mybir.EngineType.Activation, mybir.EngineType.DVE}):
             pieces = [(0, BANK), (BANK, BANK)]
             for c0, n in pieces:
@@ -329,8 +354,7 @@ def tile_decoder_k_kernel(
             for c0, n in pieces:
                 loss_log(c0, n)
             nc.scalar.activation(out=table_sb[:], in_=off[:, PIXELS_A - 1 : PIXELS_A], func=ACT.Sigmoid)
-            for c0, n in pieces:
-                loss_sum(c0, n)
+            loss_sum(0, BANK)
             for i in range(GROUPS, len(loads) - 2):
                 multiply(i)
             b2_last = b2_all[:, PIXELS_A:PIXELS]
@@ -342,6 +366,7 @@ def tile_decoder_k_kernel(
             multiply(len(loads) - 1)
             for c0, n in pieces:
                 loss_sigmoid(c0, n, acc_last[c0][:, 0:n])
+            loss_sum(BANK, BANK)
             for c0, n in pieces:
                 loss_log(c0, n)
             for c0, n in pieces:

@@ -67,8 +67,8 @@ def tile_decoder_k_kernel(
         eps_col = keep.tile([P, 1], F32)
         nc.vector.memset(eps_col[:], EPS)
 
-        w1_planes = keep.tile([P, UNITS // PLANES], U8, align_bytes=64)
-        w2_planes = keep.tile([P, GROUPS // PLANES, PIXELS], U8, align_bytes=64)
+        w1_planes = keep.tile([P, UNITS // PLANES], U8, align_bytes=256)
+        w2_planes = keep.tile([P, GROUPS // PLANES, PIXELS], U8, align_bytes=256)
         bias_rows = keep.tile([P, K_PASS], BF16)
         nc.vector.memset(w1_planes[:].bitcast(I32), 0)
         nc.vector.memset(bias_rows[:], 0.0)
@@ -79,18 +79,18 @@ def tile_decoder_k_kernel(
         n_digits = digits.shape[2]
         nc.scalar.dma_start(out=cat_sb[:, 0:n_digits], in_=digits.rearrange("s b d -> (s b) d"))
         nc.scalar.dma_start(out=cat_sb[:, n_digits:P], in_=styles.rearrange("s b d -> (s b) d"))
-        wh_sb = keep.tile([P, HIDDEN], BF16)
+        wh_sb = keep.tile([P, HIDDEN], BF16, align_bytes=256)
         nc.scalar.dma_start(out=wh_sb[:], in_=W_h)
         nc.scalar.dma_start(out=bias_rows[0:GROUPS, :], in_=b1.rearrange("(g k) -> g k", k=K_PASS))
         nc.scalar.dma_start(out=bias_rows[ROW_BH : ROW_BH + 1, :], in_=b_h.rearrange("(g k) -> g k", k=K_PASS))
         nc.scalar.dma_start(
             out=bias_rows[ROW_B2 : ROW_B2 + PIXELS // K_PASS, :], in_=b2.rearrange("(g k) -> g k", k=K_PASS)
         )
-        img_sb = keep.tile([P, PIXELS], BF16)
+        img_sb = keep.tile([P, PIXELS], BF16, align_bytes=256)
         nc.scalar.dma_start(out=img_sb[:], in_=images.rearrange("s b c h w -> (s b) (c h w)"))
         img_off = keep.tile([P, PIXELS], F32)
 
-        w1_words = keep.tile([P, UNITS], U32, align_bytes=64)
+        w1_words = keep.tile([P, UNITS], U32, align_bytes=256)
 
         def load_w1_chunk(c):
             cols = slice(c * W1_CHUNK, (c + 1) * W1_CHUNK)
@@ -128,7 +128,7 @@ def tile_decoder_k_kernel(
             if i >= len(loads):
                 return
             first, n_groups, pixel0, n_pixels = loads[i]
-            w2_tile = stream.tile([P, n_groups, n_pixels], U32, name="w2_tile", tag="w2", align_bytes=64)
+            w2_tile = stream.tile([P, n_groups, n_pixels], U32, name="w2_tile", tag="w2", align_bytes=256)
             nc.sync.dma_start(
                 out=w2_tile[:].bitcast(I32),
                 in_=w2_dram[:, first : first + n_groups, pixel0 : pixel0 + n_pixels],

@@ -37,7 +37,8 @@ GROUPS_WHOLE = 14
 GROUPS_PER_END_LOAD = 2
 GROUPS_LAST = 2
 STREAM_BUFS = 12
-LAG = 8
+LAG_FIRST = 8
+LAG_LAST = 3
 
 ROW_BH = GROUPS
 ROW_B2 = GROUPS + 1
@@ -70,19 +71,19 @@ def tile_decoder_k_kernel(
         w1_planes = keep.tile([P, UNITS // PLANES], U8, align_bytes=256)
         w2_planes = keep.tile([P, GROUPS // PLANES, PIXELS], U8, align_bytes=256)
         bias_rows = keep.tile([P, K_PASS], BF16)
-        nc.vector.memset(w1_planes[:].bitcast(I32), 0)
         nc.vector.memset(bias_rows[:], 0.0)
+        nc.vector.memset(w1_planes[:].bitcast(I32), 0)
         for i in range(GROUPS // PLANES):
             nc.vector.memset(w2_planes[:, i, :].bitcast(I32), 0)
 
         cat_sb = keep.tile([P, P], BF16)
         n_digits = digits.shape[2]
-        nc.scalar.dma_start(out=cat_sb[:, 0:n_digits], in_=digits.rearrange("s b d -> (s b) d"))
-        nc.scalar.dma_start(out=cat_sb[:, n_digits:P], in_=styles.rearrange("s b d -> (s b) d"))
+        nc.sync.dma_start(out=cat_sb[:, 0:n_digits], in_=digits.rearrange("s b d -> (s b) d"))
+        nc.sync.dma_start(out=cat_sb[:, n_digits:P], in_=styles.rearrange("s b d -> (s b) d"))
         wh_sb = keep.tile([P, HIDDEN], BF16, align_bytes=256)
-        nc.scalar.dma_start(out=wh_sb[:], in_=W_h)
-        nc.scalar.dma_start(out=bias_rows[0:GROUPS, :], in_=b1.rearrange("(g k) -> g k", k=K_PASS))
+        nc.sync.dma_start(out=wh_sb[:], in_=W_h)
         nc.scalar.dma_start(out=bias_rows[ROW_BH : ROW_BH + 1, :], in_=b_h.rearrange("(g k) -> g k", k=K_PASS))
+        nc.scalar.dma_start(out=bias_rows[0:GROUPS, :], in_=b1.rearrange("(g k) -> g k", k=K_PASS))
         nc.scalar.dma_start(
             out=bias_rows[ROW_B2 : ROW_B2 + PIXELS // K_PASS, :], in_=b2.rearrange("(g k) -> g k", k=K_PASS)
         )
@@ -138,34 +139,6 @@ def tile_decoder_k_kernel(
         for i in range(STREAM_BUFS):
             load_w2(i)
 
-        bias_sorted = keep.tile([P, PACK, P], BF16)
-        nc.vector.tensor_copy(out=bias_sorted[:], in_=bias_rows[:].rearrange("g (p j) -> g j p", j=PACK))
-        bias_ps = psum_u.tile([P, PACK, P], BF16, name="bias_ps", tag="u_ps")
-        for j in range(PACK):
-            nc.tensor.transpose(bias_ps[:, j, :], bias_sorted[:, j, :], ident_bf[:])
-        b1_exp = keep.tile([P, PACK, GROUPS], F32)
-        nc.vector.tensor_scalar(
-            out=b1_exp[:], in0=bias_ps[:, :, 0:GROUPS], scalar1=math.log(SELU_FLOOR), scalar2=None, op0=ALU.add
-        )
-        b1_relu = keep.tile([P, PACK, GROUPS], F32)
-        nc.vector.tensor_scalar(
-            out=b1_relu[:], in0=bias_ps[:, :, 0:GROUPS], scalar1=SELU_SCALE, scalar2=None, op0=ALU.mult
-        )
-        bh_col = keep.tile([P, PACK], F32)
-        nc.vector.tensor_copy(out=bh_col[:], in_=bias_ps[:, :, ROW_BH])
-
-        b2_all = keep.tile([P, PIXELS], F32)
-        for i in range(PIXELS // BANK):
-            b2_ps = psum_b.tile([P, BANK], F32, name="b2_ps", tag="b_ps")
-            nc.tensor.matmul(
-                out=b2_ps[:],
-                lhsT=ident_bf[:, ROW_B2 + i : ROW_B2 + i + 1].to_broadcast([P, P]),
-                rhs=bias_rows[:],
-                start=True,
-                stop=True,
-            )
-            nc.scalar.copy(out=b2_all[:, i * BANK : (i + 1) * BANK], in_=b2_ps[:])
-
         cat_ps = psum_u.tile([P, P], BF16, name="cat_ps", tag="u_ps")
         nc.tensor.transpose(cat_ps[:], cat_sb[:], ident_bf[:])
         catT_sb = keep.tile([P, P], BF16)
@@ -175,6 +148,14 @@ def tile_decoder_k_kernel(
         h_ps = psum_u.tile([P, PACK, P], F32, name="h_ps", tag="u_ps")
         for j in range(PACK):
             nc.tensor.matmul(out=h_ps[:, j, :], lhsT=wh_sorted[:, j, :], rhs=catT_sb[:], start=True, stop=True)
+
+        bias_sorted = keep.tile([P, PACK, P], BF16)
+        nc.vector.tensor_copy(out=bias_sorted[:], in_=bias_rows[:].rearrange("g (p j) -> g j p", j=PACK))
+        bias_ps = psum_u.tile([P, PACK, P], BF16, name="bias_ps", tag="u_ps")
+        for j in range(PACK):
+            nc.tensor.transpose(bias_ps[:, j, :], bias_sorted[:, j, :], ident_bf[:])
+        bh_col = keep.tile([P, PACK], F32)
+        nc.vector.tensor_copy(out=bh_col[:], in_=bias_ps[:, :, ROW_BH])
         h_f32 = keep.tile([P, PACK, P], F32)
         for j in range(PACK):
             nc.vector.tensor_scalar(
@@ -188,6 +169,27 @@ def tile_decoder_k_kernel(
         nc.vector.quantize_mx(
             out=h_codes[:].bitcast(FP8X4), scales=h_plane[:], in_=h_bf[:].rearrange("p m j -> p (m j)")
         )
+
+        b1_exp = keep.tile([P, PACK, GROUPS], F32)
+        nc.vector.tensor_scalar(
+            out=b1_exp[:], in0=bias_ps[:, :, 0:GROUPS], scalar1=math.log(SELU_FLOOR), scalar2=None, op0=ALU.add
+        )
+        b1_relu = keep.tile([P, PACK, GROUPS], F32)
+        nc.vector.tensor_scalar(
+            out=b1_relu[:], in0=bias_ps[:, :, 0:GROUPS], scalar1=SELU_SCALE, scalar2=None, op0=ALU.mult
+        )
+
+        b2_all = keep.tile([P, PIXELS], F32)
+        for i in range(PIXELS // BANK):
+            b2_ps = psum_b.tile([P, BANK], F32, name="b2_ps", tag="b_ps")
+            nc.tensor.matmul(
+                out=b2_ps[:],
+                lhsT=ident_bf[:, ROW_B2 + i : ROW_B2 + i + 1].to_broadcast([P, P]),
+                rhs=bias_rows[:],
+                start=True,
+                stop=True,
+            )
+            nc.scalar.copy(out=b2_all[:, i * BANK : (i + 1) * BANK], in_=b2_ps[:])
 
         t_codes = keep.tile([P, GROUPS, P], U32, align_bytes=64)
         t_planes = keep.tile([P, GROUPS, P], U8, align_bytes=64)
@@ -293,41 +295,41 @@ def tile_decoder_k_kernel(
             load_w2(i + STREAM_BUFS)
 
         loss = keep.tile([P, PIXELS // ROW], F32)
-        sums = keep.tile([P, PIXELS // ROW], F32)
-        on = keep.tile([P, PIXELS], F32)
-        off = keep.tile([P, PIXELS], F32)
+        logs = keep.tile([P, 2, PIXELS], F32)
 
         def loss_sigmoid(c0, n, sums_ps):
             cols = slice(c0, c0 + n)
-            nc.vector.tensor_tensor(out=off[:, cols], in0=sums_ps, in1=b2_all[:, cols], op=ALU.add)
-            nc.scalar.activation(out=on[:, cols], in_=off[:, cols], func=ACT.Sigmoid)
-            nc.scalar.activation(out=off[:, cols], in_=off[:, cols], func=ACT.Sigmoid, scale=-1.0)
+            nc.vector.tensor_tensor(out=logs[:, 0, cols], in0=sums_ps, in1=b2_all[:, cols], op=ALU.add)
+            nc.scalar.activation(out=logs[:, 1, cols], in_=logs[:, 0, cols], func=ACT.Sigmoid, scale=-1.0)
+            nc.scalar.activation(out=logs[:, 0, cols], in_=logs[:, 0, cols], func=ACT.Sigmoid)
 
         def loss_log(c0, n):
             cols = slice(c0, c0 + n)
-            nc.scalar.activation(out=on[:, cols], in_=on[:, cols], func=ACT.Ln, bias=eps_col[:])
-            nc.scalar.activation(out=off[:, cols], in_=off[:, cols], func=ACT.Ln, bias=eps_col[:])
+            for half in range(2):
+                nc.scalar.activation(out=logs[:, half, cols], in_=logs[:, half, cols], func=ACT.Ln, bias=eps_col[:])
 
         def loss_sum(c0, n):
             cols = slice(c0, c0 + n)
-            rows = slice(c0 // ROW, (c0 + n) // ROW)
-            nc.vector.tensor_tensor(out=on[:, cols], in0=on[:, cols], in1=img_sb[:, cols], op=ALU.mult)
+            for half, weight in ((0, img_sb), (1, img_off)):
+                nc.vector.tensor_tensor(
+                    out=logs[:, half, cols], in0=logs[:, half, cols], in1=weight[:, cols], op=ALU.mult
+                )
             nc.vector.tensor_reduce(
-                out=sums[:, rows], in_=on[:, cols].rearrange("m (r w) -> m r w", w=ROW), axis=AXIS.X, op=ALU.add
+                out=loss[:, c0 // ROW : (c0 + n) // ROW],
+                in_=logs[:, :, cols].rearrange("m h (r w) -> m r h w", w=ROW),
+                axis=AXIS.XY,
+                op=ALU.add,
             )
-            nc.vector.tensor_tensor(out=off[:, cols], in0=off[:, cols], in1=img_off[:, cols], op=ALU.mult)
-            nc.vector.tensor_reduce(
-                out=loss[:, rows], in_=off[:, cols].rearrange("m (r w) -> m r w", w=ROW), axis=AXIS.X, op=ALU.add
-            )
-            nc.vector.scalar_tensor_tensor(
-                out=loss[:, rows], in0=loss[:, rows], scalar=-1.0, in1=sums[:, rows], op0=ALU.mult, op1=ALU.subtract
-            )
+
+        def last_layer_step(g):
+            return LAG_FIRST + g * (GROUPS - 1 + LAG_LAST - LAG_FIRST) // (GROUPS - 1)
 
         with tc.manual_schedule(engines={mybir.EngineType.PE, mybir.EngineType.Activation, mybir.EngineType.DVE}):
             sort_w1(0)
             sort_w1(1)
             project(0)
-            for step in range(GROUPS + LAG):
+            g_next = 0
+            for step in range(GROUPS + LAG_LAST):
                 if step + 1 < GROUPS:
                     project(step + 1)
                 if step < GROUPS:
@@ -340,11 +342,11 @@ def tile_decoder_k_kernel(
                     sort_w1(step + 2)
                 if 0 <= step - 1 < GROUPS:
                     interleave(step - 1)
-                if step - LAG >= 0:
-                    multiply(step - LAG)
-        nc.vector.tensor_scalar(
-            out=img_off[:], in0=img_sb[:], scalar1=-1.0, scalar2=1.0, op0=ALU.mult, op1=ALU.add
-        )
+                while g_next < GROUPS and last_layer_step(g_next) <= step:
+                    multiply(g_next)
+                    g_next += 1
+        nc.vector.tensor_scalar(out=img_off[:], in0=img_sb[:], scalar1=1.0, scalar2=None, op0=ALU.subtract)
+        nc.vector.tensor_scalar(out=img_sb[:], in0=img_sb[:], scalar1=-1.0, scalar2=None, op0=ALU.mult)
         table_sb = keep.tile([P, 1], F32)
         nc.scalar.activation(out=table_sb[:], in_=e_tiles[GROUPS - 1][:, 0, 0:1], func=ACT.Sigmoid)
         with tc.manual_schedule(engines={mybir.EngineType.PE, mybir.EngineType.Activation, mybir.EngineType.DVE}):
@@ -353,7 +355,7 @@ def tile_decoder_k_kernel(
                 loss_sigmoid(c0, n, acc[c0 // BANK][:])
             for c0, n in pieces:
                 loss_log(c0, n)
-            nc.scalar.activation(out=table_sb[:], in_=off[:, PIXELS_A - 1 : PIXELS_A], func=ACT.Sigmoid)
+            nc.scalar.activation(out=table_sb[:], in_=logs[:, 1, PIXELS_A - 1 : PIXELS_A], func=ACT.Sigmoid)
             loss_sum(0, BANK)
             for i in range(GROUPS, len(loads) - 2):
                 multiply(i)

@@ -37,7 +37,7 @@ GROUPS_WHOLE = 14
 GROUPS_PER_END_LOAD = 2
 GROUPS_LAST = 2
 STREAM_BUFS = 12
-LAG_FIRST = 8
+LAG_FIRST = 12
 LAG_LAST = 3
 
 ROW_BH = GROUPS
@@ -73,8 +73,7 @@ def tile_decoder_k_kernel(
         bias_rows = keep.tile([P, K_PASS], BF16)
         nc.vector.memset(bias_rows[:], 0.0)
         nc.vector.memset(w1_planes[:].bitcast(I32), 0)
-        for i in range(GROUPS // PLANES):
-            nc.vector.memset(w2_planes[:, i, :].bitcast(I32), 0)
+        nc.gpsimd.memset(w2_planes[:].bitcast(I32), 0)
 
         cat_sb = keep.tile([P, P], BF16)
         n_digits = digits.shape[2]
@@ -107,11 +106,12 @@ def tile_decoder_k_kernel(
         for c in range(2, UNITS // W1_CHUNK):
             load_w1_chunk(c)
 
-        for s in range(GROUPS // PLANES):
-            for quad in range(4):
+        w2_scale_rows = w2_scales_dram.rearrange("(s k) q c -> q k s c", k=PLANES)
+        for quad in range(4):
+            for r in range(4):
+                first = 32 * quad + r
                 nc.gpsimd.dma_start(
-                    out=w2_planes[32 * quad : 32 * quad + 16, s, :].bitcast(F32),
-                    in_=w2_scales_dram[PLANES * s : PLANES * (s + 1), 4 * quad : 4 * quad + 4, :],
+                    out=w2_planes[first : first + 4 * PLANES : 4, :, :].bitcast(F32), in_=w2_scale_rows[4 * quad + r]
                 )
 
         loads = []
@@ -322,7 +322,9 @@ def tile_decoder_k_kernel(
             )
 
         def last_layer_step(g):
-            return LAG_FIRST + g * (GROUPS - 1 + LAG_LAST - LAG_FIRST) // (GROUPS - 1)
+            words = g * PIXELS if g < GROUPS_WHOLE else GROUPS_WHOLE * PIXELS + (g - GROUPS_WHOLE) * PIXELS_A
+            words_last = GROUPS_WHOLE * PIXELS + (GROUPS - 1 - GROUPS_WHOLE) * PIXELS_A
+            return LAG_FIRST + words * (GROUPS - 1 + LAG_LAST - LAG_FIRST) // words_last
 
         with tc.manual_schedule(engines={mybir.EngineType.PE, mybir.EngineType.Activation, mybir.EngineType.DVE}):
             sort_w1(0)

import math
from contextlib import ExitStack

import concourse.mybir as mybir
from concourse.masks import make_identity

F32 = mybir.dt.float32
BF16 = mybir.dt.bfloat16
I32 = mybir.dt.int32
U32 = mybir.dt.uint32
U8 = mybir.dt.uint8
FP8X4 = mybir.dt.float8_e4m3fn_x4
ACT = mybir.ActivationFunctionType
ALU = mybir.AluOpType
AXIS = mybir.AxisListType

P = 128
PACK = 4
K_PASS = P * PACK
BANK = 512
HIDDEN = 512
UNITS = 16384
PIXELS = 1536
ROW = 32
GROUPS = UNITS // K_PASS
EPS = 1e-9

SELU_ALPHA = 1.6732632423543772848170429916717
SELU_SCALE = 1.0507009873554804934193349852946
SELU_FLOOR = SELU_SCALE * SELU_ALPHA

PLANES = 4
W1_CHUNK = 2048
W1_PLANE_COLS = 1024
PIXELS_A = 1024
GROUPS_WHOLE = 14
GROUPS_PER_END_LOAD = 2
GROUPS_LAST = 2
STREAM_BUFS = 12
LAG_FIRST = 12
LAG_LAST = 3

ROW_BH = GROUPS
ROW_B2 = GROUPS + 1

FLOPS = 2 * P * (P * HIDDEN + HIDDEN * UNITS + UNITS * PIXELS)


def tile_decoder_k_kernel(
    tc, digits, styles, images, W_h, b_h, W1_words, W1_scales, b1, W2_words, W2_scales, b2, out
):
    nc = tc.nc
    with ExitStack() as ctx:
        keep = ctx.enter_context(tc.tile_pool(name="keep", bufs=1))
        stream = ctx.enter_context(tc.tile_pool(name="stream", bufs=STREAM_BUFS))
        work = ctx.enter_context(tc.tile_pool(name="work", bufs=3))
        psum_acc = ctx.enter_context(tc.psum_pool(name="psum_acc", bufs=1))
        psum_b = ctx.enter_context(tc.psum_pool(name="psum_b", bufs=2))
        psum_u = ctx.enter_context(tc.psum_pool(name="psum_u", bufs=3))

        w1_dram = W1_words[0].rearrange("p n t -> p (n t)").bitcast(I32)
        w1_scales_dram = W1_scales[0].bitcast(I32)
        w2_dram = W2_words.rearrange("g p n t -> p g (n t)").bitcast(I32)
        w2_scales_dram = W2_scales.bitcast(F32)

        ident_bf = keep.tile([P, P], BF16)
        make_identity(nc, ident_bf[:])
        eps_col = keep.tile([P, 1], F32)
        nc.vector.memset(eps_col[:], EPS)

        w1_planes = keep.tile([P, UNITS // PLANES], U8, align_bytes=256)
        w2_planes = keep.tile([P, GROUPS // PLANES, PIXELS], U8, align_bytes=256)
        bias_rows = keep.tile([P, K_PASS], BF16)
        nc.vector.memset(bias_rows[:], 0.0)
        nc.vector.memset(w1_planes[:].bitcast(I32), 0)
        nc.gpsimd.memset(w2_planes[:].bitcast(I32), 0)

        cat_sb = keep.tile([P, P], BF16)
        n_digits = digits.shape[2]
        nc.sync.dma_start(out=cat_sb[:, 0:n_digits], in_=digits.rearrange("s b d -> (s b) d"))
        nc.sync.dma_start(out=cat_sb[:, n_digits:P], in_=styles.rearrange("s b d -> (s b) d"))
        wh_sb = keep.tile([P, HIDDEN], BF16, align_bytes=256)
        nc.sync.dma_start(out=wh_sb[:], in_=W_h)
        nc.scalar.dma_start(out=bias_rows[ROW_BH : ROW_BH + 1, :], in_=b_h.rearrange("(g k) -> g k", k=K_PASS))
        nc.scalar.dma_start(out=bias_rows[0:GROUPS, :], in_=b1.rearrange("(g k) -> g k", k=K_PASS))
        nc.scalar.dma_start(
            out=bias_rows[ROW_B2 : ROW_B2 + PIXELS // K_PASS, :], in_=b2.rearrange("(g k) -> g k", k=K_PASS)
        )
        img_sb = keep.tile([P, PIXELS], BF16, align_bytes=256)
        nc.scalar.dma_start(out=img_sb[:], in_=images.rearrange("s b c h w -> (s b) (c h w)"))
        img_off = keep.tile([P, PIXELS], F32)

        w1_words = keep.tile([P, UNITS], U32, align_bytes=256)

        def load_w1_chunk(c):
            cols = slice(c * W1_CHUNK, (c + 1) * W1_CHUNK)
            nc.sync.dma_start(out=w1_words[:, cols].bitcast(I32), in_=w1_dram[:, cols])

        load_w1_chunk(0)
        load_w1_chunk(1)
        for quad in range(4):
            nc.sync.dma_start(
                out=w1_planes[32 * quad : 32 * quad + 16, :].bitcast(I32),
                in_=w1_scales_dram[4 * quad : 4 * quad + 4, :].rearrange("r (k c) -> k r c", k=PLANES),
            )
        for c in range(2, UNITS // W1_CHUNK):
            load_w1_chunk(c)

        w2_scale_rows = w2_scales_dram.rearrange("(s k) q c -> q k s c", k=PLANES)
        for quad in range(4):
            for r in range(4):
                first = 32 * quad + r
                nc.gpsimd.dma_start(
                    out=w2_planes[first : first + 4 * PLANES : 4, :, :].bitcast(F32), in_=w2_scale_rows[4 * quad + r]
                )

        loads = []
        for g in range(GROUPS_WHOLE):
            loads.append((g, 1, 0, PIXELS))
        for g in range(GROUPS_WHOLE, GROUPS):
            loads.append((g, 1, 0, PIXELS_A))
        for first in range(GROUPS_WHOLE, GROUPS - GROUPS_LAST, GROUPS_PER_END_LOAD):
            loads.append((first, GROUPS_PER_END_LOAD, PIXELS_A, BANK))
        for pixel0 in range(PIXELS_A, PIXELS, BANK // 2):
            loads.append((GROUPS - GROUPS_LAST, GROUPS_LAST, pixel0, BANK // 2))
        w2_tiles = {}

        def load_w2(i):
            if i >= len(loads):
                return
            first, n_groups, pixel0, n_pixels = loads[i]
            w2_tile = stream.tile([P, n_groups, n_pixels], U32, name="w2_tile", tag="w2", align_bytes=256)
            nc.sync.dma_start(
                out=w2_tile[:].bitcast(I32),
                in_=w2_dram[:, first : first + n_groups, pixel0 : pixel0 + n_pixels],
            )
            w2_tiles[i] = w2_tile

        for i in range(STREAM_BUFS):
            load_w2(i)

        cat_ps = psum_u.tile([P, P], BF16, name="cat_ps", tag="u_ps")
        nc.tensor.transpose(cat_ps[:], cat_sb[:], ident_bf[:])
        catT_sb = keep.tile([P, P], BF16)
        nc.vector.tensor_copy(out=catT_sb[:], in_=cat_ps[:])
        wh_sorted = keep.tile([P, PACK, P], BF16)
        nc.vector.tensor_copy(out=wh_sorted[:], in_=wh_sb[:].rearrange("c (p j) -> c j p", j=PACK))
        h_ps = psum_u.tile([P, PACK, P], F32, name="h_ps", tag="u_ps")
        for j in range(PACK):
            nc.tensor.matmul(out=h_ps[:, j, :], lhsT=wh_sorted[:, j, :], rhs=catT_sb[:], start=True, stop=True)

        bias_sorted = keep.tile([P, PACK, P], BF16)
        nc.vector.tensor_copy(out=bias_sorted[:], in_=bias_rows[:].rearrange("g (p j) -> g j p", j=PACK))
        bias_ps = psum_u.tile([P, PACK, P], BF16, name="bias_ps", tag="u_ps")
        for j in range(PACK):
            nc.tensor.transpose(bias_ps[:, j, :], bias_sorted[:, j, :], ident_bf[:])
        bh_col = keep.tile([P, PACK], F32)
        nc.vector.tensor_copy(out=bh_col[:], in_=bias_ps[:, :, ROW_BH])
        h_f32 = keep.tile([P, PACK, P], F32)
        for j in range(PACK):
            nc.vector.tensor_scalar(
                out=h_f32[:, j, :], in0=h_ps[:, j, :], scalar1=bh_col[:, j : j + 1], scalar2=0.0,
                op0=ALU.add, op1=ALU.max,
            )
        h_bf = keep.tile([P, P, PACK], BF16, align_bytes=64)
        nc.vector.tensor_copy(out=h_bf[:], in_=h_f32[:].rearrange("p j m -> p m j"))
        h_codes = keep.tile([P, P], U32, align_bytes=64)
        h_plane = keep.tile([P, P], U8, align_bytes=64)
        nc.vector.quantize_mx(
            out=h_codes[:].bitcast(FP8X4), scales=h_plane[:], in_=h_bf[:].rearrange("p m j -> p (m j)")
        )

        b1_exp = keep.tile([P, PACK, GROUPS], F32)
        nc.vector.tensor_scalar(
            out=b1_exp[:], in0=bias_ps[:, :, 0:GROUPS], scalar1=math.log(SELU_FLOOR), scalar2=None, op0=ALU.add
        )
        b1_relu = keep.tile([P, PACK, GROUPS], F32)
        nc.vector.tensor_scalar(
            out=b1_relu[:], in0=bias_ps[:, :, 0:GROUPS], scalar1=SELU_SCALE, scalar2=None, op0=ALU.mult
        )

        b2_all = keep.tile([P, PIXELS], F32)
        for i in range(PIXELS // BANK):
            b2_ps = psum_b.tile([P, BANK], F32, name="b2_ps", tag="b_ps")
            nc.tensor.matmul(
                out=b2_ps[:],
                lhsT=ident_bf[:, ROW_B2 + i : ROW_B2 + i + 1].to_broadcast([P, P]),
                rhs=bias_rows[:],
                start=True,
                stop=True,
            )
            nc.scalar.copy(out=b2_all[:, i * BANK : (i + 1) * BANK], in_=b2_ps[:])

        t_codes = keep.tile([P, GROUPS, P], U32, align_bytes=64)
        t_planes = keep.tile([P, GROUPS, P], U8, align_bytes=64)
        w1_planes_sorted = keep.tile([P, UNITS // PLANES], U8, align_bytes=64)
        units_per_plane = UNITS // PLANES

        def sort_w1_planes(col0):
            cols = slice(col0, col0 + W1_PLANE_COLS)
            nc.vector.tensor_copy(
                out=w1_planes_sorted[:, cols].rearrange("q (g j p) -> q g j p", j=PACK, p=P),
                in_=w1_planes[:, cols].rearrange("q (g p j) -> q g j p", j=PACK, p=P),
            )

        sorted_tiles, u_tiles, e_tiles, r_tiles, t_tiles, in_tiles = {}, {}, {}, {}, {}, {}

        def sort_w1(g):
            unit0 = g * K_PASS
            if unit0 < units_per_plane and unit0 % W1_PLANE_COLS == 0:
                sort_w1_planes(unit0)
            w1_sorted = work.tile([P, PACK, P], U32, name="w1_sorted", align_bytes=64)
            nc.vector.tensor_copy(
                out=w1_sorted[:].bitcast(I32),
                in_=w1_words[:, unit0 : unit0 + K_PASS].bitcast(I32).rearrange("q (p j) -> q j p", j=PACK),
            )
            sorted_tiles[g] = w1_sorted

        def project(g):
            unit0 = g * K_PASS
            offset = 4 * (unit0 // units_per_plane)
            col0 = unit0 % units_per_plane
            u_ps = psum_u.tile([P, PACK, P], F32, name="u_ps", tag="u_ps")
            for j in range(PACK):
                nc.tensor.matmul_mx(
                    out=u_ps[:, j, :],
                    lhsT=sorted_tiles[g][:, j, :].bitcast(FP8X4),
                    lhsT_scale=w1_planes_sorted[offset:P, col0 + j * P : col0 + (j + 1) * P],
                    rhs=h_codes[:].bitcast(FP8X4),
                    rhs_scale=h_plane[:],
                    start=True,
                    stop=True,
                )
            u_tiles[g] = u_ps

        def activate(g):
            e_sb = work.tile([P, PACK, P], F32, name="e_sb")
            r_sb = work.tile([P, PACK, P], BF16, name="r_sb")
            for j in range(PACK):
                nc.scalar.activation(
                    out=e_sb[:, j, :], in_=u_tiles[g][:, j, :], func=ACT.Exp, bias=b1_exp[:, j, g : g + 1], scale=1.0
                )
                nc.scalar.activation(
                    out=r_sb[:, j, :], in_=u_tiles[g][:, j, :], func=ACT.Relu, bias=b1_relu[:, j, g : g + 1],
                    scale=SELU_SCALE,
                )
            e_tiles[g], r_tiles[g] = e_sb, r_sb

        def join(g):
            t_bf = work.tile([P, PACK, P], BF16, name="t_bf")
            nc.vector.scalar_tensor_tensor(
                out=t_bf[:], in0=e_tiles[g][:], scalar=SELU_FLOOR, in1=r_tiles[g][:], op0=ALU.subtract, op1=ALU.min
            )
            t_tiles[g] = t_bf

        def interleave(g):
            t_in = work.tile([P, P, PACK], BF16, name="t_in", align_bytes=64)
            nc.vector.tensor_copy(out=t_in[:], in_=t_tiles[g][:].rearrange("p j m -> p m j"))
            in_tiles[g] = t_in

        def quantize(g):
            nc.vector.quantize_mx(
                out=t_codes[:, g, :].bitcast(FP8X4),
                scales=t_planes[:, g, :],
                in_=in_tiles[g][:].rearrange("p m j -> p (m j)"),
            )

        acc = []
        for bank in range(PIXELS // BANK):
            acc.append(psum_acc.tile([P, BANK], F32, name="acc%d" % bank))
        acc_last = {}

        def multiply(i):
            first, n_groups, pixel0, n_pixels = loads[i]
            for gi in range(n_groups):
                g = first + gi
                width = min(n_pixels, BANK)
                for col0 in range(0, n_pixels, width):
                    pixel = pixel0 + col0
                    if width == BANK:
                        acc_cols = acc[pixel // BANK][:]
                        g_start, g_stop = 0, GROUPS - 1 if pixel < PIXELS_A else GROUPS - GROUPS_LAST - 1
                    else:
                        acc_cols = acc_last[pixel][:, 0:width]
                        g_start, g_stop = GROUPS - GROUPS_LAST, GROUPS - 1
                    nc.tensor.matmul_mx(
                        out=acc_cols,
                        lhsT=t_codes[:, g, :].bitcast(FP8X4),
                        lhsT_scale=t_planes[:, g, :],
                        rhs=w2_tiles[i][:, gi, col0 : col0 + width].bitcast(FP8X4),
                        rhs_scale=w2_planes[4 * (g % PLANES) : P, g // PLANES, pixel : pixel + width],
                        start=(g == g_start),
                        stop=(g == g_stop),
                    )
            load_w2(i + STREAM_BUFS)

        loss = keep.tile([P, PIXELS // ROW], F32)
        logs = keep.tile([P, 2, PIXELS], F32)

        def loss_sigmoid(c0, n, sums_ps):
            cols = slice(c0, c0 + n)
            nc.vector.tensor_tensor(out=logs[:, 0, cols], in0=sums_ps, in1=b2_all[:, cols], op=ALU.add)
            nc.scalar.activation(out=logs[:, 1, cols], in_=logs[:, 0, cols], func=ACT.Sigmoid, scale=-1.0)
            nc.scalar.activation(out=logs[:, 0, cols], in_=logs[:, 0, cols], func=ACT.Sigmoid)

        def loss_log(c0, n):
            cols = slice(c0, c0 + n)
            for half in range(2):
                nc.scalar.activation(out=logs[:, half, cols], in_=logs[:, half, cols], func=ACT.Ln, bias=eps_col[:])

        def loss_sum(c0, n):
            cols = slice(c0, c0 + n)
            for half, weight in ((0, img_sb), (1, img_off)):
                nc.vector.tensor_tensor(
                    out=logs[:, half, cols], in0=logs[:, half, cols], in1=weight[:, cols], op=ALU.mult
                )
            nc.vector.tensor_reduce(
                out=loss[:, c0 // ROW : (c0 + n) // ROW],
                in_=logs[:, :, cols].rearrange("m h (r w) -> m r h w", w=ROW),
                axis=AXIS.XY,
                op=ALU.add,
            )

        def last_layer_step(g):
            words = g * PIXELS if g < GROUPS_WHOLE else GROUPS_WHOLE * PIXELS + (g - GROUPS_WHOLE) * PIXELS_A
            words_last = GROUPS_WHOLE * PIXELS + (GROUPS - 1 - GROUPS_WHOLE) * PIXELS_A
            return LAG_FIRST + words * (GROUPS - 1 + LAG_LAST - LAG_FIRST) // words_last

        with tc.manual_schedule(engines={mybir.EngineType.PE, mybir.EngineType.Activation, mybir.EngineType.DVE}):
            sort_w1(0)
            sort_w1(1)
            project(0)
            g_next = 0
            for step in range(GROUPS + LAG_LAST):
                if step + 1 < GROUPS:
                    project(step + 1)
                if step < GROUPS:
                    activate(step)
                if 0 <= step - 1 < GROUPS:
                    join(step - 1)
                if 0 <= step - 2 < GROUPS:
                    quantize(step - 2)
                if step + 2 < GROUPS:
                    sort_w1(step + 2)
                if 0 <= step - 1 < GROUPS:
                    interleave(step - 1)
                while g_next < GROUPS and last_layer_step(g_next) <= step:
                    multiply(g_next)
                    g_next += 1
        nc.vector.tensor_scalar(out=img_off[:], in0=img_sb[:], scalar1=1.0, scalar2=None, op0=ALU.subtract)
        nc.vector.tensor_scalar(out=img_sb[:], in0=img_sb[:], scalar1=-1.0, scalar2=None, op0=ALU.mult)
        table_sb = keep.tile([P, 1], F32)
        nc.scalar.activation(out=table_sb[:], in_=e_tiles[GROUPS - 1][:, 0, 0:1], func=ACT.Sigmoid)
        with tc.manual_schedule(engines={mybir.EngineType.PE, mybir.EngineType.Activation, mybir.EngineType.DVE}):
            pieces = [(0, BANK), (BANK, BANK)]
            for c0, n in pieces:
                loss_sigmoid(c0, n, acc[c0 // BANK][:])
            for c0, n in pieces:
                loss_log(c0, n)
            nc.scalar.activation(out=table_sb[:], in_=logs[:, 1, PIXELS_A - 1 : PIXELS_A], func=ACT.Sigmoid)
            loss_sum(0, BANK)
            for i in range(GROUPS, len(loads) - 2):
                multiply(i)
            b2_last = b2_all[:, PIXELS_A:PIXELS]
            nc.vector.tensor_tensor(out=b2_last, in0=acc[PIXELS_A // BANK][:], in1=b2_last, op=ALU.add)
            pieces = [(PIXELS_A, BANK // 2), (PIXELS_A + BANK // 2, BANK // 2)]
            for c0, n in pieces:
                acc_last[c0] = psum_b.tile([P, BANK], F32, name="acc_last", tag="b_ps")
            multiply(len(loads) - 2)
            multiply(len(loads) - 1)
            for c0, n in pieces:
                loss_sigmoid(c0, n, acc_last[c0][:, 0:n])
            loss_sum(BANK, BANK)
            for c0, n in pieces:
                loss_log(c0, n)
            for c0, n in pieces:
                loss_sum(c0, n)
            nc.sync.dma_start(out=out.rearrange("s b c h -> (s b) (c h)"), in_=loss[:])
